import numpy as np
import ml_dtypes


def mxq(x, axis, fmt="e4m3"):
    dtype, down = {"e4m3": (ml_dtypes.float8_e4m3fn, 7), "e5m2": (ml_dtypes.float8_e5m2, 14)}[fmt]
    v = np.moveaxis(np.asarray(x, np.float32).astype(ml_dtypes.bfloat16).astype(np.float64), axis, -1)
    blocks = v.reshape(v.shape[:-1] + (-1, 32))
    amax = np.abs(blocks).max(-1, keepdims=True)
    byte = np.maximum(np.where(amax > 0, np.frexp(amax)[1] - 1 + 127, 0) - down, 1)
    scale = np.exp2(byte - 127.0)
    codes = (blocks / scale).astype(np.float32).astype(dtype).astype(np.float64)
    return np.moveaxis((codes * scale).reshape(v.shape), -1, axis)


WIDE = False


def mx_kscale(k):
    if not WIDE:
        return np.ones(k)
    levels = np.array([10, -10, 5, -5, 0])
    a = np.random.permutation(np.resize(levels, k // 512 * 4)).reshape(k // 512, 4)
    idx = np.arange(k)
    return np.exp2(a[idx // 512, idx % 128 // 32])


BF16 = ml_dtypes.bfloat16


def bf(x):
    return np.asarray(x, np.float32).astype(BF16)


def f64(x):
    return np.asarray(x).astype(np.float64)


E2M1 = np.array([0.0, 0.5, 1.0, 1.5, 2.0, 3.0, 4.0, 6.0, -0.0, -0.5, -1.0, -1.5, -2.0, -3.0, -4.0, -6.0])


def pack_weight(w, fmt):
    k, n = w.shape
    w = f64(bf(w)).reshape(k // 32, 32, n)
    amax = np.abs(w).max(1)
    if fmt == "e4m3":
        byte = np.frexp(amax)[1] - 1 + 127 - 7
    else:
        mant, ex = np.frexp(amax / 6.0)
        byte = np.where(mant > 0.5, ex, ex - 1) + 127
    byte = np.clip(np.where(amax > 0, byte, 1), 1, 254)
    scaled = (w * np.exp2(127.0 - byte)[:, None, :]).reshape(k, n).astype(np.float32)
    by_word = np.ascontiguousarray(scaled.reshape(k // 512, 128, 4, n).transpose(0, 1, 3, 2))
    if fmt == "e4m3":
        words = by_word.astype(ml_dtypes.float8_e4m3fn).view(np.uint8)
    else:
        c = by_word.astype(ml_dtypes.float4_e2m1fn).view(np.uint8) & 0xF
        words = c[..., 0::2] | (c[..., 1::2] << 4)
    return np.ascontiguousarray(words), np.ascontiguousarray(byte.astype(np.uint8).reshape(k // 512, 16, n))


def unpack_weight(words, scales, fmt):
    g, p, n, _ = words.shape
    if fmt == "e4m3":
        vals = np.ascontiguousarray(words).view(ml_dtypes.float8_e4m3fn).astype(np.float64)
    else:
        nib = np.empty((g, p, n, 4), np.uint8)
        nib[..., 0::2] = words & 0xF
        nib[..., 1::2] = words >> 4
        vals = E2M1[nib]
    vals = vals * np.repeat(np.exp2(scales.astype(np.float64) - 127.0), 8, axis=1)[..., None]
    return vals.transpose(0, 1, 3, 2).reshape(g * 512, n)

def pack4(w):
    words, scales = pack_weight(w, "e2m1")
    return words.reshape(words.shape[0], 128, -1), scales


def unpack4(words, scales):
    return unpack_weight(words.reshape(words.shape[0], 128, -1, 2), scales, "e2m1")


B, S, D, E, HD = 4, 1024, 512, 1024, 64
ROPE_BASE = 10000.0


def rope_tables():
    inv_freq = 1.0 / ROPE_BASE ** (np.arange(0, E, 2) / E)
    ang = np.repeat(np.arange(S)[:, None] * inv_freq[None, :], 2, axis=-1)
    return np.cos(ang), np.sin(ang)


def rotate_half(v):
    h = v.shape[-1] // 2
    return np.concatenate([-v[..., h:], v[..., :h]], axis=-1)


def setup_inputs():
    s = mx_kscale(D)
    x = bf(np.random.standard_normal((B, S, D)) * s)
    Wq_words, Wq_scales = pack4(np.random.standard_normal((D, E)) * 0.5 / np.sqrt(D) / s[:, None])
    bq = bf(np.random.standard_normal(E) * 0.1)
    Wk_words, Wk_scales = pack4(np.random.standard_normal((D, E)) * 0.5 / np.sqrt(D) / s[:, None])
    bk = bf(np.random.standard_normal(E) * 0.1)
    return {"x": x,
            "Wq_words": Wq_words,
            "Wq_scales": Wq_scales,
            "bq": bq,
            "Wk_words": Wk_words,
            "Wk_scales": Wk_scales,
            "bk": bk}


def reference(x, Wq_words, Wq_scales, bq, Wk_words, Wk_scales, bk):
    xq = mxq(f64(x), 2, "e4m3")
    q = (xq @ unpack4(Wq_words, Wq_scales)) + f64(bq)
    k = (xq @ unpack4(Wk_words, Wk_scales)) + f64(bk)
    cos, sin = rope_tables()
    qr = q * cos + rotate_half(q) * sin
    kr = k * cos + rotate_half(k) * sin
    return qr, kr

@@ -1,0 +1,247 @@
+import math
+from contextlib import ExitStack
+
+import concourse.mybir as mybir
+from concourse.masks import make_identity
+
+F32 = mybir.dt.float32
+BF16 = mybir.dt.bfloat16
+I32 = mybir.dt.int32
+U32 = mybir.dt.uint32
+U8 = mybir.dt.uint8
+FP8X4 = mybir.dt.float8_e4m3fn_x4
+FP4X4 = mybir.dt.float4_e2m1fn_x4
+ALU = mybir.AluOpType
+ACT = mybir.ActivationFunctionType
+
+P = 128
+BATCH, SEQ, DIM, FEAT = 4, 1024, 512, 1024
+ROPE_BASE = 10000.0
+TOKENS = 512
+BLOCKS = TOKENS // P
+SPANS = SEQ // TOKENS
+PAIRS = FEAT // (2 * P)
+WORDS = DIM // 2
+
+FLOPS = 2 * BATCH * SEQ * DIM * 2 * FEAT
+
+
+def tile_ropemultiheadattention_pa_t_kernel(
+    tc, x, Wq_words, Wq_scales, bq, Wk_words, Wk_scales, bk, out_0, out_1
+):
+    nc = tc.nc
+    outs = (out_0, out_1)
+
+    with ExitStack() as pools:
+        const = pools.enter_context(tc.tile_pool(name="const", bufs=1))
+        angle = pools.enter_context(tc.tile_pool(name="angle", bufs=2))
+        x_in = pools.enter_context(tc.tile_pool(name="x_in", bufs=3))
+        x_mx = pools.enter_context(tc.tile_pool(name="x_mx", bufs=2))
+        rotated = pools.enter_context(tc.tile_pool(name="rotated", bufs=3))
+        staging = pools.enter_context(tc.tile_pool(name="staging", bufs=3))
+
+        groups = [(batch, span) for span in range(SPANS) for batch in range(BATCH)]
+
+        def load_x(g):
+            batch, span = groups[g]
+            rows = x[batch, span * TOKENS : (span + 1) * TOKENS, :]
+            x_rows = x_in.tile([P, BLOCKS, DIM], BF16)
+            nc.sync.dma_start(out=x_rows[:], in_=rows.rearrange("(n p) k -> p n k", p=P))
+            return x_rows
+
+        loaded = {0: load_x(0)}
+
+        w_words = const.tile([P, 2, 2 * FEAT], U8, align_bytes=64)
+        w_scales = const.tile([P, 2, FEAT], U8, align_bytes=64)
+        nc.vector.memset(w_scales[:].bitcast(I32), 0)
+        for proj, (words, scales) in enumerate(((Wq_words, Wq_scales), (Wk_words, Wk_scales))):
+            nc.sync.dma_start(out=w_words[:, proj, :].bitcast(I32), in_=words[0].bitcast(I32))
+            for quad in range(4):
+                nc.sync.dma_start(
+                    out=w_scales[32 * quad : 32 * quad + 4, proj, :].bitcast(I32),
+                    in_=scales[0, 4 * quad : 4 * quad + 4, :].bitcast(I32),
+                )
+
+        ident = const.tile([P, P], F32)
+        make_identity(nc, ident[:])
+
+        tiles = FEAT // P
+        bias_rows = const.tile([P, P], BF16)
+        nc.vector.memset(bias_rows[:], 0.0)
+        nc.sync.dma_start(out=bias_rows[0:tiles, :], in_=bq.rearrange("(t p) -> t p", p=P))
+        nc.sync.dma_start(out=bias_rows[tiles : 2 * tiles, :], in_=bk.rearrange("(t p) -> t p", p=P))
+        bias_rows_f32 = const.tile([P, P], F32)
+        nc.vector.tensor_copy(out=bias_rows_f32[:], in_=bias_rows[:])
+
+        ratio = ROPE_BASE ** (-2.0 / FEAT)
+        ratio_row = const.tile([P, P], F32)
+        nc.vector.memset(ratio_row[:, 0:2], 1.0)
+        width = 2
+        while width < P:
+            nc.vector.tensor_scalar_mul(
+                out=ratio_row[:, width : 2 * width],
+                in0=ratio_row[:, 0:width],
+                scalar1=ratio ** (width // 2),
+            )
+            width *= 2
+
+        bias = const.tile([P, 2 * tiles], F32)
+        turns = const.tile([P, PAIRS, 2], F32)
+        with tc.psum_pool(name="setup_ps", bufs=1) as setup_ps:
+            turned = setup_ps.tile([P, 2, P], F32)
+            nc.tensor.transpose(turned[:, 0, :], bias_rows_f32[:], ident[:])
+            nc.tensor.transpose(turned[:, 1, :], ratio_row[:], ident[:])
+            nc.vector.tensor_copy(out=bias[:], in_=turned[:, 0, 0 : 2 * tiles])
+            for h in range(PAIRS):
+                for j in range(2):
+                    first = ratio ** ((PAIRS * j + h) * P // 2) / (2.0 * math.pi)
+                    nc.vector.tensor_scalar_mul(
+                        out=turns[:, h, j : j + 1],
+                        in0=turned[:, 1, 0:1],
+                        scalar1=first if j == 1 else -first,
+                    )
+
+        position = const.tile([P, SEQ], F32)
+        nc.vector.memset(position[:, 0:1], 0.0)
+        width = 1
+        while width < SEQ:
+            nc.vector.tensor_scalar_add(
+                out=position[:, width : 2 * width], in0=position[:, 0:width], scalar1=float(width)
+            )
+            width *= 2
+
+        quarter = const.tile([P, 1], F32)
+        nc.vector.memset(quarter[:], 0.25)
+        quarter_turn = const.tile([P, 1], F32)
+        nc.vector.tensor_scalar_mul(out=quarter_turn[:], in0=quarter[:], scalar1=2.0 * math.pi)
+
+        cos_table = const.tile([P, PAIRS, 2, SEQ], F32)
+        sin_table = const.tile([P, PAIRS, 2, SEQ], F32)
+
+        def build_tables(span, h):
+            cols = slice(span * TOKENS, (span + 1) * TOKENS)
+            whole = angle.tile([P, 2, TOKENS], I32)
+            part = angle.tile([P, 2, TOKENS], F32)
+            for j in range(2):
+                nc.vector.tensor_scalar_mul(
+                    out=whole[:, j, :], in0=position[:, cols], scalar1=turns[:, h, j : j + 1]
+                )
+                nc.vector.scalar_tensor_tensor(
+                    out=part[:, j, :],
+                    in0=position[:, cols],
+                    scalar=turns[:, h, j : j + 1],
+                    in1=whole[:, j, :],
+                    op0=ALU.mult,
+                    op1=ALU.subtract,
+                )
+            nc.scalar.activation(
+                out=sin_table[:, h, :, cols], in_=part[:], func=ACT.Sin, scale=2.0 * math.pi
+            )
+            size = angle.tile([P, 2, TOKENS], F32)
+            nc.scalar.activation(out=size[:], in_=part[:], func=ACT.Abs)
+            nc.scalar.activation(
+                out=cos_table[:, h, :, cols],
+                in_=size[:],
+                func=ACT.Sin,
+                scale=-2.0 * math.pi,
+                bias=quarter_turn[:, 0:1],
+            )
+
+        x_ps = pools.enter_context(tc.psum_pool(name="x_ps", bufs=2))
+        mx_ps = pools.enter_context(tc.psum_pool(name="mx_ps", bufs=2))
+        sum_ps = pools.enter_context(tc.psum_pool(name="sum_ps", bufs=2))
+
+        def quantise_x(x_rows):
+            grouped = x_mx.tile([P, 4 * TOKENS], BF16, align_bytes=64)
+            grouped_words = grouped[:].bitcast(F32).rearrange(
+                "p (c n m u) -> p c n m u", c=BLOCKS // 2, n=2, u=2
+            )
+            for c in range(BLOCKS // 2):
+                planes = x_ps.tile([P, 2, 2, P], F32)
+                for n in range(2):
+                    words = x_rows[:, 2 * c + n, :].bitcast(F32)
+                    for u in range(2):
+                        nc.tensor.transpose(planes[:, n, u, :], words[:, u:WORDS:2], ident[:])
+                nc.scalar.copy(
+                    out=grouped_words[:, c], in_=planes[:].rearrange("p n u m -> p n m u")
+                )
+            codes = x_mx.tile([P, TOKENS], U32, align_bytes=64)
+            scales = x_mx.tile([P, TOKENS], U8, align_bytes=64)
+            nc.vector.quantize_mx(out=codes[:].bitcast(FP8X4), scales=scales[:], in_=grouped[:])
+            return codes, scales
+
+        def project(x_group, proj, h):
+            codes, scales = x_group
+            lower = mx_ps.tile([P, TOKENS], F32)
+            upper = mx_ps.tile([P, TOKENS], F32)
+            for j, bank in enumerate((lower, upper)):
+                t = PAIRS * j + h
+                nc.tensor.matmul_mx(
+                    out=bank[:],
+                    lhsT=w_words[:, proj, 2 * P * t : 2 * P * (t + 1)].bitcast(FP4X4),
+                    lhsT_scale=w_scales[:, proj, P * t : P * (t + 1)],
+                    rhs=codes[:].bitcast(FP8X4),
+                    rhs_scale=scales[:],
+                    start=True,
+                    stop=True,
+                )
+            return lower, upper
+
+        def rotate(banks, span, proj, h, stage):
+            cols = slice(span * TOKENS, (span + 1) * TOKENS)
+            products = rotated.tile([P, 2, 2, TOKENS], F32)
+            for j in range(2):
+                for term, table in enumerate((cos_table, sin_table)):
+                    source = j if term == 0 else 1 - j
+                    t = tiles * proj + PAIRS * source + h
+                    nc.vector.scalar_tensor_tensor(
+                        out=products[:, j, term, :],
+                        in0=banks[source][:],
+                        scalar=bias[:, t : t + 1],
+                        in1=table[:, h, j, cols],
+                        op0=ALU.add,
+                        op1=ALU.mult,
+                    )
+            for j in range(2):
+                sums = sum_ps.tile([P, BLOCKS, P], F32)
+                for n in range(BLOCKS):
+                    for term in range(2):
+                        nc.tensor.matmul(
+                            out=sums[:, n, :],
+                            lhsT=products[:, j, term, n * P : (n + 1) * P],
+                            rhs=ident[:],
+                            is_transpose=True,
+                            start=(term == 0),
+                            stop=(term == 1),
+                        )
+                t = PAIRS * j + h
+                nc.scalar.copy(out=stage[:, :, t * P : (t + 1) * P], in_=sums[:])
+
+        steps = [(g, proj, h) for g in range(len(groups)) for proj in range(2) for h in range(PAIRS)]
+
+        loaded[1] = load_x(1)
+        x_group = quantise_x(loaded[0])
+        x_next = x_group
+        build_tables(0, 0)
+        banks_next = project(x_group, 0, 0)
+        stage = None
+        for i, (g, proj, h) in enumerate(steps):
+            batch, span = groups[g]
+            banks = banks_next
+            if proj == 0 and h == 0 and g + 2 < len(groups):
+                loaded[g + 2] = load_x(g + 2)
+            if proj == 1 and h == 0 and g + 1 < len(groups):
+                x_next = quantise_x(loaded[g + 1])
+            if i + 1 < len(steps):
+                g1, proj1, h1 = steps[i + 1]
+                if g1 != g:
+                    x_group = x_next
+                if groups[g1][0] == 0 and proj1 == 0:
+                    build_tables(groups[g1][1], h1)
+                banks_next = project(x_group, proj1, h1)
+            if h == 0:
+                stage = staging.tile([P, BLOCKS, FEAT], F32)
+            rotate(banks, span, proj, h, stage)
+            if h == PAIRS - 1:
+                rows = outs[proj][batch, span * TOKENS : (span + 1) * TOKENS, :]
+                nc.sync.dma_start(out=rows.rearrange("(n p) i -> p n i", p=P), in_=stage[:])

@@ -37,7 +37,8 @@ def tile_ropemultiheadattention_pa_t_kernel(
         angle = pools.enter_context(tc.tile_pool(name="angle", bufs=2))
         x_in = pools.enter_context(tc.tile_pool(name="x_in", bufs=3))
         x_mx = pools.enter_context(tc.tile_pool(name="x_mx", bufs=2))
-        rotated = pools.enter_context(tc.tile_pool(name="rotated", bufs=3))
+        rotated = pools.enter_context(tc.tile_pool(name="rotated", bufs=4))
+        lifted = pools.enter_context(tc.tile_pool(name="lifted", bufs=2))
         staging = pools.enter_context(tc.tile_pool(name="staging", bufs=3))
 
         groups = [(batch, span) for span in range(SPANS) for batch in range(BATCH)]
@@ -187,12 +188,34 @@ def tile_ropemultiheadattention_pa_t_kernel(
                 )
             return lower, upper
 
-        def rotate(banks, span, proj, h, stage):
+        def shared_products(banks, span, proj, h):
             cols = slice(span * TOKENS, (span + 1) * TOKENS)
             products = rotated.tile([P, 2, 2, TOKENS], F32)
+            t = tiles * proj + h
+            lower_sb = lifted.tile([P, TOKENS], F32)
+            nc.scalar.activation(
+                out=lower_sb[:], in_=banks[0][:], func=ACT.Identity, bias=bias[:, t : t + 1], scale=1.0
+            )
+            nc.gpsimd.tensor_tensor(
+                out=products[:, 0, 0, :], in0=lower_sb[:], in1=cos_table[:, h, 0, cols], op=ALU.mult
+            )
+            nc.gpsimd.tensor_tensor(
+                out=products[:, 1, 1, :], in0=lower_sb[:], in1=sin_table[:, h, 1, cols], op=ALU.mult
+            )
+            return products
+
+        def vector_products(banks, span, proj, h, products):
+            cols = slice(span * TOKENS, (span + 1) * TOKENS)
+            sources = (0, 1)
+            if products is None:
+                products = rotated.tile([P, 2, 2, TOKENS], F32)
+            else:
+                sources = (1,)
             for j in range(2):
                 for term, table in enumerate((cos_table, sin_table)):
                     source = j if term == 0 else 1 - j
+                    if source not in sources:
+                        continue
                     t = tiles * proj + PAIRS * source + h
                     nc.vector.scalar_tensor_tensor(
                         out=products[:, j, term, :],
@@ -202,6 +225,9 @@ def tile_ropemultiheadattention_pa_t_kernel(
                         op0=ALU.add,
                         op1=ALU.mult,
                     )
+            return products
+
+        def turn_back(products, h, stage):
             for j in range(2):
                 sums = sum_ps.tile([P, BLOCKS, P], F32)
                 for n in range(BLOCKS):
@@ -219,29 +245,45 @@ def tile_ropemultiheadattention_pa_t_kernel(
 
         steps = [(g, proj, h) for g in range(len(groups)) for proj in range(2) for h in range(PAIRS)]
 
+        def builds_tables(step):
+            g, proj, h = step
+            return groups[g][0] == 0 and proj == 0
+
+        def is_shared(i):
+            return i % 2 == 1 and not builds_tables(steps[i])
+
         loaded[1] = load_x(1)
         x_group = quantise_x(loaded[0])
         x_next = x_group
         build_tables(0, 0)
-        banks_next = project(x_group, 0, 0)
-        stage = None
-        for i, (g, proj, h) in enumerate(steps):
-            batch, span = groups[g]
-            banks = banks_next
-            if proj == 0 and h == 0 and g + 2 < len(groups):
-                loaded[g + 2] = load_x(g + 2)
-            if proj == 1 and h == 0 and g + 1 < len(groups):
-                x_next = quantise_x(loaded[g + 1])
+        banks_of = {0: project(x_group, 0, 0)}
+        products_of = {0: None}
+        stages = {}
+        for i in range(len(steps) + 1):
+            if i < len(steps):
+                g, proj, h = steps[i]
+                if proj == 0 and h == 0 and g + 2 < len(groups):
+                    loaded[g + 2] = load_x(g + 2)
+                if proj == 1 and h == 0 and g + 1 < len(groups):
+                    x_next = quantise_x(loaded[g + 1])
             if i + 1 < len(steps):
                 g1, proj1, h1 = steps[i + 1]
                 if g1 != g:
                     x_group = x_next
-                if groups[g1][0] == 0 and proj1 == 0:
+                if builds_tables(steps[i + 1]):
                     build_tables(groups[g1][1], h1)
-                banks_next = project(x_group, proj1, h1)
-            if h == 0:
-                stage = staging.tile([P, BLOCKS, FEAT], F32)
-            rotate(banks, span, proj, h, stage)
-            if h == PAIRS - 1:
-                rows = outs[proj][batch, span * TOKENS : (span + 1) * TOKENS, :]
-                nc.sync.dma_start(out=rows.rearrange("(n p) i -> p n i", p=P), in_=stage[:])
+                banks_of[i + 1] = project(x_group, proj1, h1)
+                products_of[i + 1] = None
+                if is_shared(i + 1):
+                    products_of[i + 1] = shared_products(banks_of[i + 1], groups[g1][1], proj1, h1)
+            if i < len(steps):
+                products_of[i] = vector_products(banks_of[i], groups[g][1], proj, h, products_of[i])
+            if i >= 1:
+                g0, proj0, h0 = steps[i - 1]
+                batch, span = groups[g0]
+                if h0 == 0:
+                    stages[0] = staging.tile([P, BLOCKS, FEAT], F32, name="stage")
+                turn_back(products_of[i - 1], h0, stages[0])
+                if h0 == PAIRS - 1:
+                    rows = outs[proj0][batch, span * TOKENS : (span + 1) * TOKENS, :]
+                    nc.sync.dma_start(out=rows.rearrange("(n p) i -> p n i", p=P), in_=stages[0][:])

@@ -88,19 +88,19 @@ def tile_ropemultiheadattention_pa_t_kernel(
 
         bias = const.tile([P, 2 * tiles], F32)
         turns = const.tile([P, PAIRS, 2], F32)
-        with tc.psum_pool(name="setup_ps", bufs=1) as setup_ps:
-            turned = setup_ps.tile([P, 2, P], F32)
-            nc.tensor.transpose(turned[:, 0, :], bias_rows_f32[:], ident[:])
-            nc.tensor.transpose(turned[:, 1, :], ratio_row[:], ident[:])
-            nc.vector.tensor_copy(out=bias[:], in_=turned[:, 0, 0 : 2 * tiles])
-            for h in range(PAIRS):
-                for j in range(2):
-                    first = ratio ** ((PAIRS * j + h) * P // 2) / (2.0 * math.pi)
-                    nc.vector.tensor_scalar_mul(
-                        out=turns[:, h, j : j + 1],
-                        in0=turned[:, 1, 0:1],
-                        scalar1=first if j == 1 else -first,
-                    )
+        keep_ps = pools.enter_context(tc.psum_pool(name="keep_ps", bufs=1))
+        turned = keep_ps.tile([P, 2, P], F32)
+        nc.tensor.transpose(turned[:, 0, :], bias_rows_f32[:], ident[:])
+        nc.tensor.transpose(turned[:, 1, :], ratio_row[:], ident[:])
+        nc.vector.tensor_copy(out=bias[:], in_=turned[:, 0, 0 : 2 * tiles])
+        for h in range(PAIRS):
+            for j in range(2):
+                first = ratio ** ((PAIRS * j + h) * P // 2) / (2.0 * math.pi)
+                nc.vector.tensor_scalar_mul(
+                    out=turns[:, h, j : j + 1],
+                    in0=turned[:, 1, 0:1],
+                    scalar1=first if j == 1 else -first,
+                )
 
         position = const.tile([P, SEQ], F32)
         nc.vector.memset(position[:, 0:1], 0.0)
@@ -148,24 +148,28 @@ def tile_ropemultiheadattention_pa_t_kernel(
                 bias=quarter_turn[:, 0:1],
             )
 
-        x_ps = pools.enter_context(tc.psum_pool(name="x_ps", bufs=2))
+        x_ps = pools.enter_context(tc.psum_pool(name="x_ps", bufs=1))
         mx_ps = pools.enter_context(tc.psum_pool(name="mx_ps", bufs=2))
         sum_ps = pools.enter_context(tc.psum_pool(name="sum_ps", bufs=2))
 
         def quantise_x(x_rows):
             grouped = x_mx.tile([P, 4 * TOKENS], BF16, align_bytes=64)
+            for c in range(BLOCKS // 2):
+                turn_x(x_rows, grouped, c)
+            return quantise(grouped)
+
+        def turn_x(x_rows, grouped, c):
             grouped_words = grouped[:].bitcast(F32).rearrange(
                 "p (c n m u) -> p c n m u", c=BLOCKS // 2, n=2, u=2
             )
-            for c in range(BLOCKS // 2):
-                planes = x_ps.tile([P, 2, 2, P], F32)
-                for n in range(2):
-                    words = x_rows[:, 2 * c + n, :].bitcast(F32)
-                    for u in range(2):
-                        nc.tensor.transpose(planes[:, n, u, :], words[:, u:WORDS:2], ident[:])
-                nc.scalar.copy(
-                    out=grouped_words[:, c], in_=planes[:].rearrange("p n u m -> p n m u")
-                )
+            planes = x_ps.tile([P, 2, 2, P], F32)
+            for n in range(2):
+                words = x_rows[:, 2 * c + n, :].bitcast(F32)
+                for u in range(2):
+                    nc.tensor.transpose(planes[:, n, u, :], words[:, u:WORDS:2], ident[:])
+            nc.scalar.copy(out=grouped_words[:, c], in_=planes[:].rearrange("p n u m -> p n m u"))
+
+        def quantise(grouped):
             codes = x_mx.tile([P, TOKENS], U32, align_bytes=64)
             scales = x_mx.tile([P, TOKENS], U8, align_bytes=64)
             nc.vector.quantize_mx(out=codes[:].bitcast(FP8X4), scales=scales[:], in_=grouped[:])
@@ -220,7 +224,7 @@ def tile_ropemultiheadattention_pa_t_kernel(
                     nc.vector.scalar_tensor_tensor(
                         out=products[:, j, term, :],
                         in0=banks[source][:],
-                        scalar=bias[:, t : t + 1],
+                        scalar=turned[:, 0, t : t + 1],
                         in1=table[:, h, j, cols],
                         op0=ALU.add,
                         op1=ALU.mult,
@@ -259,13 +263,19 @@ def tile_ropemultiheadattention_pa_t_kernel(
         banks_of = {0: project(x_group, 0, 0)}
         products_of = {0: None}
         stages = {}
+        halves = {}
         for i in range(len(steps) + 1):
             if i < len(steps):
                 g, proj, h = steps[i]
                 if proj == 0 and h == 0 and g + 2 < len(groups):
                     loaded[g + 2] = load_x(g + 2)
-                if proj == 1 and h == 0 and g + 1 < len(groups):
-                    x_next = quantise_x(loaded[g + 1])
+                if proj == 1 and g + 1 < len(groups):
+                    if h == 0:
+                        halves[0] = x_mx.tile([P, 4 * TOKENS], BF16, align_bytes=64, name="grouped")
+                    if h < BLOCKS // 2:
+                        turn_x(loaded[g + 1], halves[0], h)
+                    if h == BLOCKS // 2:
+                        x_next = quantise(halves[0])
             if i + 1 < len(steps):
                 g1, proj1, h1 = steps[i + 1]
                 if g1 != g:

@@ -148,9 +148,8 @@ def tile_ropemultiheadattention_pa_t_kernel(
                 bias=quarter_turn[:, 0:1],
             )
 
-        x_ps = pools.enter_context(tc.psum_pool(name="x_ps", bufs=1))
         mx_ps = pools.enter_context(tc.psum_pool(name="mx_ps", bufs=2))
-        sum_ps = pools.enter_context(tc.psum_pool(name="sum_ps", bufs=2))
+        turn_ps = pools.enter_context(tc.psum_pool(name="turn_ps", bufs=3))
 
         def quantise_x(x_rows):
             grouped = x_mx.tile([P, 4 * TOKENS], BF16, align_bytes=64)
@@ -162,7 +161,7 @@ def tile_ropemultiheadattention_pa_t_kernel(
             grouped_words = grouped[:].bitcast(F32).rearrange(
                 "p (c n m u) -> p c n m u", c=BLOCKS // 2, n=2, u=2
             )
-            planes = x_ps.tile([P, 2, 2, P], F32)
+            planes = turn_ps.tile([P, 2, 2, P], F32, name="bank", tag="bank")
             for n in range(2):
                 words = x_rows[:, 2 * c + n, :].bitcast(F32)
                 for u in range(2):
@@ -232,20 +231,23 @@ def tile_ropemultiheadattention_pa_t_kernel(
             return products
 
         def turn_back(products, h, stage):
+            sums = {}
             for j in range(2):
-                sums = sum_ps.tile([P, BLOCKS, P], F32)
-                for n in range(BLOCKS):
-                    for term in range(2):
+                sums[j] = turn_ps.tile([P, BLOCKS, P], F32, name="bank", tag="bank")
+            for n in range(BLOCKS):
+                for term in range(2):
+                    for j in range(2):
                         nc.tensor.matmul(
-                            out=sums[:, n, :],
+                            out=sums[j][:, n, :],
                             lhsT=products[:, j, term, n * P : (n + 1) * P],
                             rhs=ident[:],
                             is_transpose=True,
                             start=(term == 0),
                             stop=(term == 1),
                         )
+            for j in range(2):
                 t = PAIRS * j + h
-                nc.scalar.copy(out=stage[:, :, t * P : (t + 1) * P], in_=sums[:])
+                nc.scalar.copy(out=stage[:, :, t * P : (t + 1) * P], in_=sums[j][:])
 
         steps = [(g, proj, h) for g in range(len(groups)) for proj in range(2) for h in range(PAIRS)]
 

@@ -22,6 +22,7 @@ BLOCKS = TOKENS // P
 SPANS = SEQ // TOKENS
 PAIRS = FEAT // (2 * P)
 WORDS = DIM // 2
+JOINED = 2
 
 FLOPS = 2 * BATCH * SEQ * DIM * 2 * FEAT
 
@@ -231,25 +232,23 @@ def tile_ropemultiheadattention_pa_t_kernel(
             return products
 
         def turn_back(products, h, stage):
-            sums = {}
             for j in range(2):
-                sums[j] = turn_ps.tile([P, BLOCKS, P], F32, name="bank", tag="bank")
-            for n in range(BLOCKS):
-                for term in range(2):
-                    for j in range(2):
+                sums = turn_ps.tile([P, BLOCKS, P], F32, name="bank", tag="bank")
+                for n in range(BLOCKS):
+                    for term in range(2):
                         nc.tensor.matmul(
-                            out=sums[j][:, n, :],
+                            out=sums[:, n, :],
                             lhsT=products[:, j, term, n * P : (n + 1) * P],
                             rhs=ident[:],
                             is_transpose=True,
                             start=(term == 0),
                             stop=(term == 1),
                         )
-            for j in range(2):
                 t = PAIRS * j + h
-                nc.scalar.copy(out=stage[:, :, t * P : (t + 1) * P], in_=sums[j][:])
+                nc.scalar.copy(out=stage[:, :, t * P : (t + 1) * P], in_=sums[:])
 
         steps = [(g, proj, h) for g in range(len(groups)) for proj in range(2) for h in range(PAIRS)]
+        per_group = 2 * PAIRS // JOINED
 
         def builds_tables(step):
             g, proj, h = step
@@ -258,44 +257,56 @@ def tile_ropemultiheadattention_pa_t_kernel(
         def is_shared(i):
             return i % 2 == 1 and not builds_tables(steps[i])
 
-        loaded[1] = load_x(1)
-        x_group = quantise_x(loaded[0])
-        x_next = x_group
-        build_tables(0, 0)
-        banks_of = {0: project(x_group, 0, 0)}
-        products_of = {0: None}
+        x_of = {}
+        banks_of = {}
+        products_of = {}
         stages = {}
         halves = {}
-        for i in range(len(steps) + 1):
-            if i < len(steps):
+
+        def front(m):
+            members = range(JOINED * m, JOINED * (m + 1))
+            for i in members:
                 g, proj, h = steps[i]
-                if proj == 0 and h == 0 and g + 2 < len(groups):
-                    loaded[g + 2] = load_x(g + 2)
-                if proj == 1 and g + 1 < len(groups):
-                    if h == 0:
-                        halves[0] = x_mx.tile([P, 4 * TOKENS], BF16, align_bytes=64, name="grouped")
-                    if h < BLOCKS // 2:
-                        turn_x(loaded[g + 1], halves[0], h)
-                    if h == BLOCKS // 2:
-                        x_next = quantise(halves[0])
-            if i + 1 < len(steps):
-                g1, proj1, h1 = steps[i + 1]
-                if g1 != g:
-                    x_group = x_next
-                if builds_tables(steps[i + 1]):
-                    build_tables(groups[g1][1], h1)
-                banks_of[i + 1] = project(x_group, proj1, h1)
-                products_of[i + 1] = None
-                if is_shared(i + 1):
-                    products_of[i + 1] = shared_products(banks_of[i + 1], groups[g1][1], proj1, h1)
-            if i < len(steps):
+                if builds_tables(steps[i]):
+                    build_tables(groups[g][1], h)
+            for i in members:
+                g, proj, h = steps[i]
+                banks_of[i] = project(x_of[g], proj, h)
+            for i in members:
+                g, proj, h = steps[i]
+                products_of[i] = None
+                if is_shared(i):
+                    products_of[i] = shared_products(banks_of[i], groups[g][1], proj, h)
+            for i in members:
+                g, proj, h = steps[i]
                 products_of[i] = vector_products(banks_of[i], groups[g][1], proj, h, products_of[i])
-            if i >= 1:
-                g0, proj0, h0 = steps[i - 1]
-                batch, span = groups[g0]
-                if h0 == 0:
+
+        def back(m):
+            for i in range(JOINED * m, JOINED * (m + 1)):
+                g, proj, h = steps[i]
+                batch, span = groups[g]
+                if h == 0:
                     stages[0] = staging.tile([P, BLOCKS, FEAT], F32, name="stage")
-                turn_back(products_of[i - 1], h0, stages[0])
-                if h0 == PAIRS - 1:
-                    rows = outs[proj0][batch, span * TOKENS : (span + 1) * TOKENS, :]
+                turn_back(products_of[i], h, stages[0])
+                if h == PAIRS - 1:
+                    rows = outs[proj][batch, span * TOKENS : (span + 1) * TOKENS, :]
                     nc.sync.dma_start(out=rows.rearrange("(n p) i -> p n i", p=P), in_=stages[0][:])
+
+        loaded[1] = load_x(1)
+        x_of[0] = quantise_x(loaded[0])
+        front(0)
+        for m in range(len(steps) // JOINED):
+            g = steps[JOINED * m][0]
+            place = m % per_group
+            if place == 0 and g + 2 < len(groups):
+                loaded[g + 2] = load_x(g + 2)
+            if g + 1 < len(groups):
+                if place == 0:
+                    halves[0] = x_mx.tile([P, 4 * TOKENS], BF16, align_bytes=64, name="grouped")
+                if place < BLOCKS // 2:
+                    turn_x(loaded[g + 1], halves[0], place)
+                if place == BLOCKS // 2:
+                    x_of[g + 1] = quantise(halves[0])
+            if m + 1 < len(steps) // JOINED:
+                front(m + 1)
+            back(m)

@@ -40,7 +40,7 @@ def tile_ropemultiheadattention_pa_t_kernel(
         x_mx = pools.enter_context(tc.tile_pool(name="x_mx", bufs=2))
         rotated = pools.enter_context(tc.tile_pool(name="rotated", bufs=4))
         lifted = pools.enter_context(tc.tile_pool(name="lifted", bufs=2))
-        staging = pools.enter_context(tc.tile_pool(name="staging", bufs=3))
+        staging = pools.enter_context(tc.tile_pool(name="staging", bufs=4))
 
         groups = [(batch, span) for span in range(SPANS) for batch in range(BATCH)]
 
@@ -120,34 +120,44 @@ def tile_ropemultiheadattention_pa_t_kernel(
         cos_table = const.tile([P, PAIRS, 2, SEQ], F32)
         sin_table = const.tile([P, PAIRS, 2, SEQ], F32)
 
-        def build_tables(span, h):
+        def table_stage(span, h, stage_no, kept):
             cols = slice(span * TOKENS, (span + 1) * TOKENS)
-            whole = angle.tile([P, 2, TOKENS], I32)
-            part = angle.tile([P, 2, TOKENS], F32)
-            for j in range(2):
-                nc.vector.tensor_scalar_mul(
-                    out=whole[:, j, :], in0=position[:, cols], scalar1=turns[:, h, j : j + 1]
+            if stage_no == 0:
+                whole = angle.tile([P, 2, TOKENS], I32)
+                part = angle.tile([P, 2, TOKENS], F32)
+                for j in range(2):
+                    nc.vector.tensor_scalar_mul(
+                        out=whole[:, j, :], in0=position[:, cols], scalar1=turns[:, h, j : j + 1]
+                    )
+                    nc.vector.scalar_tensor_tensor(
+                        out=part[:, j, :],
+                        in0=position[:, cols],
+                        scalar=turns[:, h, j : j + 1],
+                        in1=whole[:, j, :],
+                        op0=ALU.mult,
+                        op1=ALU.subtract,
+                    )
+                nc.scalar.activation(
+                    out=sin_table[:, h, :, cols], in_=part[:], func=ACT.Sin, scale=2.0 * math.pi
                 )
-                nc.vector.scalar_tensor_tensor(
-                    out=part[:, j, :],
-                    in0=position[:, cols],
-                    scalar=turns[:, h, j : j + 1],
-                    in1=whole[:, j, :],
-                    op0=ALU.mult,
-                    op1=ALU.subtract,
+                kept[0] = part
+            if stage_no == 1:
+                size = angle.tile([P, 2, TOKENS], F32)
+                nc.scalar.activation(out=size[:], in_=kept[0][:], func=ACT.Abs)
+                kept[1] = size
+            if stage_no == 2:
+                nc.scalar.activation(
+                    out=cos_table[:, h, :, cols],
+                    in_=kept[1][:],
+                    func=ACT.Sin,
+                    scale=-2.0 * math.pi,
+                    bias=quarter_turn[:, 0:1],
                 )
-            nc.scalar.activation(
-                out=sin_table[:, h, :, cols], in_=part[:], func=ACT.Sin, scale=2.0 * math.pi
-            )
-            size = angle.tile([P, 2, TOKENS], F32)
-            nc.scalar.activation(out=size[:], in_=part[:], func=ACT.Abs)
-            nc.scalar.activation(
-                out=cos_table[:, h, :, cols],
-                in_=size[:],
-                func=ACT.Sin,
-                scale=-2.0 * math.pi,
-                bias=quarter_turn[:, 0:1],
-            )
+
+        def build_tables(span, h):
+            kept = {}
+            for stage_no in range(3):
+                table_stage(span, h, stage_no, kept)
 
         mx_ps = pools.enter_context(tc.psum_pool(name="mx_ps", bufs=2))
         turn_ps = pools.enter_context(tc.psum_pool(name="turn_ps", bufs=3))
@@ -231,44 +241,49 @@ def tile_ropemultiheadattention_pa_t_kernel(
                     )
             return products
 
-        def turn_back(products, h, stage):
+        def add_first_half(products):
+            nc.gpsimd.tensor_tensor(
+                out=products[:, 0, 0, :], in0=products[:, 0, 0, :], in1=products[:, 0, 1, :], op=ALU.add
+            )
+
+        def turn_back(products, h, stage, summed):
             for j in range(2):
                 sums = turn_ps.tile([P, BLOCKS, P], F32, name="bank", tag="bank")
+                terms = 1 if (summed and j == 0) else 2
                 for n in range(BLOCKS):
-                    for term in range(2):
+                    for term in range(terms):
                         nc.tensor.matmul(
                             out=sums[:, n, :],
                             lhsT=products[:, j, term, n * P : (n + 1) * P],
                             rhs=ident[:],
                             is_transpose=True,
                             start=(term == 0),
-                            stop=(term == 1),
+                            stop=(term == terms - 1),
                         )
                 t = PAIRS * j + h
                 nc.scalar.copy(out=stage[:, :, t * P : (t + 1) * P], in_=sums[:])
 
-        steps = [(g, proj, h) for g in range(len(groups)) for proj in range(2) for h in range(PAIRS)]
+        steps = [(0, proj, h) for h in range(PAIRS) for proj in range(2)]
+        steps.extend(
+            (g, proj, h) for g in range(1, len(groups)) for proj in range(2) for h in range(PAIRS)
+        )
         per_group = 2 * PAIRS // JOINED
 
-        def builds_tables(step):
-            g, proj, h = step
-            return groups[g][0] == 0 and proj == 0
-
         def is_shared(i):
-            return i % 2 == 1 and not builds_tables(steps[i])
+            return i % 2 == 0
+
+        def is_summed(i):
+            return i % 2 == 1
 
         x_of = {}
         banks_of = {}
         products_of = {}
         stages = {}
         halves = {}
+        later = {}
 
         def front(m):
             members = range(JOINED * m, JOINED * (m + 1))
-            for i in members:
-                g, proj, h = steps[i]
-                if builds_tables(steps[i]):
-                    build_tables(groups[g][1], h)
             for i in members:
                 g, proj, h = steps[i]
                 banks_of[i] = project(x_of[g], proj, h)
@@ -280,21 +295,26 @@ def tile_ropemultiheadattention_pa_t_kernel(
             for i in members:
                 g, proj, h = steps[i]
                 products_of[i] = vector_products(banks_of[i], groups[g][1], proj, h, products_of[i])
+            for i in members:
+                if is_summed(i):
+                    add_first_half(products_of[i])
 
         def back(m):
             for i in range(JOINED * m, JOINED * (m + 1)):
                 g, proj, h = steps[i]
                 batch, span = groups[g]
                 if h == 0:
-                    stages[0] = staging.tile([P, BLOCKS, FEAT], F32, name="stage")
-                turn_back(products_of[i], h, stages[0])
+                    stages[proj] = staging.tile([P, BLOCKS, FEAT], F32, name="stage")
+                turn_back(products_of[i], h, stages[proj], is_summed(i))
                 if h == PAIRS - 1:
                     rows = outs[proj][batch, span * TOKENS : (span + 1) * TOKENS, :]
-                    nc.sync.dma_start(out=rows.rearrange("(n p) i -> p n i", p=P), in_=stages[0][:])
+                    nc.sync.dma_start(out=rows.rearrange("(n p) i -> p n i", p=P), in_=stages[proj][:])
 
         loaded[1] = load_x(1)
         x_of[0] = quantise_x(loaded[0])
+        build_tables(0, 0)
         front(0)
+        build_tables(0, 1)
         for m in range(len(steps) // JOINED):
             g = steps[JOINED * m][0]
             place = m % per_group
@@ -307,6 +327,10 @@ def tile_ropemultiheadattention_pa_t_kernel(
                     turn_x(loaded[g + 1], halves[0], place)
                 if place == BLOCKS // 2:
                     x_of[g + 1] = quantise(halves[0])
+            if m + 2 < PAIRS:
+                build_tables(0, m + 2)
+            if per_group <= m < per_group + 3 * PAIRS:
+                table_stage(1, (m - per_group) // 3, (m - per_group) % 3, later)
             if m + 1 < len(steps) // JOINED:
                 front(m + 1)
             back(m)

@@ -22,6 +22,7 @@ BLOCKS = TOKENS // P
 SPANS = SEQ // TOKENS
 PAIRS = FEAT // (2 * P)
 WORDS = DIM // 2
+SUMMED = 1
 JOINED = 2
 
 FLOPS = 2 * BATCH * SEQ * DIM * 2 * FEAT
@@ -117,8 +118,7 @@ def tile_ropemultiheadattention_pa_t_kernel(
         quarter_turn = const.tile([P, 1], F32)
         nc.vector.tensor_scalar_mul(out=quarter_turn[:], in0=quarter[:], scalar1=2.0 * math.pi)
 
-        cos_table = const.tile([P, PAIRS, 2, SEQ], F32)
-        sin_table = const.tile([P, PAIRS, 2, SEQ], F32)
+        table = const.tile([P, PAIRS, 2, 2, SEQ], F32)
 
         def table_stage(span, h, stage_no, kept):
             cols = slice(span * TOKENS, (span + 1) * TOKENS)
@@ -137,9 +137,10 @@ def tile_ropemultiheadattention_pa_t_kernel(
                         op0=ALU.mult,
                         op1=ALU.subtract,
                     )
-                nc.scalar.activation(
-                    out=sin_table[:, h, :, cols], in_=part[:], func=ACT.Sin, scale=2.0 * math.pi
-                )
+                for j in range(2):
+                    nc.scalar.activation(
+                        out=table[:, h, 1 - j, j, cols], in_=part[:, j, :], func=ACT.Sin, scale=2.0 * math.pi
+                    )
                 kept[0] = part
             if stage_no == 1:
                 size = angle.tile([P, 2, TOKENS], F32)
@@ -147,7 +148,7 @@ def tile_ropemultiheadattention_pa_t_kernel(
                 kept[1] = size
             if stage_no == 2:
                 nc.scalar.activation(
-                    out=cos_table[:, h, :, cols],
+                    out=table[:, h].rearrange("p a b s -> p (a b) s")[:, 0:4:3, cols],
                     in_=kept[1][:],
                     func=ACT.Sin,
                     scale=-2.0 * math.pi,
@@ -211,10 +212,10 @@ def tile_ropemultiheadattention_pa_t_kernel(
                 out=lower_sb[:], in_=banks[0][:], func=ACT.Identity, bias=bias[:, t : t + 1], scale=1.0
             )
             nc.gpsimd.tensor_tensor(
-                out=products[:, 0, 0, :], in0=lower_sb[:], in1=cos_table[:, h, 0, cols], op=ALU.mult
-            )
-            nc.gpsimd.tensor_tensor(
-                out=products[:, 1, 1, :], in0=lower_sb[:], in1=sin_table[:, h, 1, cols], op=ALU.mult
+                out=products[:, 0, :, :],
+                in0=lower_sb[:].unsqueeze(1).to_broadcast([P, 2, TOKENS]),
+                in1=table[:, h, 0, :, cols],
+                op=ALU.mult,
             )
             return products
 
@@ -225,40 +226,39 @@ def tile_ropemultiheadattention_pa_t_kernel(
                 products = rotated.tile([P, 2, 2, TOKENS], F32)
             else:
                 sources = (1,)
-            for j in range(2):
-                for term, table in enumerate((cos_table, sin_table)):
-                    source = j if term == 0 else 1 - j
-                    if source not in sources:
-                        continue
-                    t = tiles * proj + PAIRS * source + h
-                    nc.vector.scalar_tensor_tensor(
-                        out=products[:, j, term, :],
-                        in0=banks[source][:],
-                        scalar=turned[:, 0, t : t + 1],
-                        in1=table[:, h, j, cols],
-                        op0=ALU.add,
-                        op1=ALU.mult,
-                    )
+            for source in sources:
+                t = tiles * proj + PAIRS * source + h
+                nc.vector.scalar_tensor_tensor(
+                    out=products[:, source, :, :],
+                    in0=banks[source][:].unsqueeze(1).to_broadcast([P, 2, TOKENS]),
+                    scalar=turned[:, 0, t : t + 1],
+                    in1=table[:, h, source, :, cols],
+                    op0=ALU.add,
+                    op1=ALU.mult,
+                )
             return products
 
-        def add_first_half(products):
+        def add_halves(products):
             nc.gpsimd.tensor_tensor(
-                out=products[:, 0, 0, :], in0=products[:, 0, 0, :], in1=products[:, 0, 1, :], op=ALU.add
+                out=products[:, 0, 0:SUMMED, :],
+                in0=products[:, 0, 0:SUMMED, :],
+                in1=products[:, 1, 0:SUMMED, :],
+                op=ALU.add,
             )
 
         def turn_back(products, h, stage, summed):
             for j in range(2):
                 sums = turn_ps.tile([P, BLOCKS, P], F32, name="bank", tag="bank")
-                terms = 1 if (summed and j == 0) else 2
+                terms = 1 if (summed and j < SUMMED) else 2
                 for n in range(BLOCKS):
-                    for term in range(terms):
+                    for source in range(terms):
                         nc.tensor.matmul(
                             out=sums[:, n, :],
-                            lhsT=products[:, j, term, n * P : (n + 1) * P],
+                            lhsT=products[:, source, j, n * P : (n + 1) * P],
                             rhs=ident[:],
                             is_transpose=True,
-                            start=(term == 0),
-                            stop=(term == terms - 1),
+                            start=(source == 0),
+                            stop=(source == terms - 1),
                         )
                 t = PAIRS * j + h
                 nc.scalar.copy(out=stage[:, :, t * P : (t + 1) * P], in_=sums[:])
@@ -297,7 +297,7 @@ def tile_ropemultiheadattention_pa_t_kernel(
                 products_of[i] = vector_products(banks_of[i], groups[g][1], proj, h, products_of[i])
             for i in members:
                 if is_summed(i):
-                    add_first_half(products_of[i])
+                    add_halves(products_of[i])
 
         def back(m):
             for i in range(JOINED * m, JOINED * (m + 1)):

@@ -20,7 +20,8 @@ ROPE_BASE = 10000.0
 TOKENS = 512
 BLOCKS = TOKENS // P
 SPANS = SEQ // TOKENS
-PAIRS = FEAT // (2 * P)
+TILES = FEAT // P
+PAIRS = TILES // 2
 WORDS = DIM // 2
 SUMMED = 1
 JOINED = 2
@@ -42,6 +43,9 @@ def tile_ropemultiheadattention_pa_t_kernel(
         rotated = pools.enter_context(tc.tile_pool(name="rotated", bufs=4))
         lifted = pools.enter_context(tc.tile_pool(name="lifted", bufs=2))
         staging = pools.enter_context(tc.tile_pool(name="staging", bufs=4))
+        keep_ps = pools.enter_context(tc.psum_pool(name="keep_ps", bufs=1))
+        mx_ps = pools.enter_context(tc.psum_pool(name="mx_ps", bufs=2))
+        turn_ps = pools.enter_context(tc.psum_pool(name="turn_ps", bufs=3))
 
         groups = [(batch, span) for span in range(SPANS) for batch in range(BATCH)]
 
@@ -53,7 +57,10 @@ def tile_ropemultiheadattention_pa_t_kernel(
             return x_rows
 
         loaded = {0: load_x(0)}
-
+        bias_rows = const.tile([P, P], BF16)
+        nc.vector.memset(bias_rows[:], 0.0)
+        nc.sync.dma_start(out=bias_rows[0:TILES, :], in_=bq.rearrange("(t p) -> t p", p=P))
+        nc.sync.dma_start(out=bias_rows[TILES : 2 * TILES, :], in_=bk.rearrange("(t p) -> t p", p=P))
         w_words = const.tile([P, 2, 2 * FEAT], U8, align_bytes=64)
         w_scales = const.tile([P, 2, FEAT], U8, align_bytes=64)
         nc.vector.memset(w_scales[:].bitcast(I32), 0)
@@ -64,17 +71,10 @@ def tile_ropemultiheadattention_pa_t_kernel(
                     out=w_scales[32 * quad : 32 * quad + 4, proj, :].bitcast(I32),
                     in_=scales[0, 4 * quad : 4 * quad + 4, :].bitcast(I32),
                 )
+        loaded[1] = load_x(1)
 
         ident = const.tile([P, P], F32)
         make_identity(nc, ident[:])
-
-        tiles = FEAT // P
-        bias_rows = const.tile([P, P], BF16)
-        nc.vector.memset(bias_rows[:], 0.0)
-        nc.sync.dma_start(out=bias_rows[0:tiles, :], in_=bq.rearrange("(t p) -> t p", p=P))
-        nc.sync.dma_start(out=bias_rows[tiles : 2 * tiles, :], in_=bk.rearrange("(t p) -> t p", p=P))
-        bias_rows_f32 = const.tile([P, P], F32)
-        nc.vector.tensor_copy(out=bias_rows_f32[:], in_=bias_rows[:])
 
         ratio = ROPE_BASE ** (-2.0 / FEAT)
         ratio_row = const.tile([P, P], F32)
@@ -88,21 +88,8 @@ def tile_ropemultiheadattention_pa_t_kernel(
             )
             width *= 2
 
-        bias = const.tile([P, 2 * tiles], F32)
-        turns = const.tile([P, PAIRS, 2], F32)
-        keep_ps = pools.enter_context(tc.psum_pool(name="keep_ps", bufs=1))
         turned = keep_ps.tile([P, 2, P], F32)
-        nc.tensor.transpose(turned[:, 0, :], bias_rows_f32[:], ident[:])
         nc.tensor.transpose(turned[:, 1, :], ratio_row[:], ident[:])
-        nc.vector.tensor_copy(out=bias[:], in_=turned[:, 0, 0 : 2 * tiles])
-        for h in range(PAIRS):
-            for j in range(2):
-                first = ratio ** ((PAIRS * j + h) * P // 2) / (2.0 * math.pi)
-                nc.vector.tensor_scalar_mul(
-                    out=turns[:, h, j : j + 1],
-                    in0=turned[:, 1, 0:1],
-                    scalar1=first if j == 1 else -first,
-                )
 
         position = const.tile([P, SEQ], F32)
         nc.vector.memset(position[:, 0:1], 0.0)
@@ -117,6 +104,16 @@ def tile_ropemultiheadattention_pa_t_kernel(
         nc.vector.memset(quarter[:], 0.25)
         quarter_turn = const.tile([P, 1], F32)
         nc.vector.tensor_scalar_mul(out=quarter_turn[:], in0=quarter[:], scalar1=2.0 * math.pi)
+
+        turns = const.tile([P, PAIRS, 2], F32)
+        for h in range(PAIRS):
+            for j in range(2):
+                first = ratio ** ((PAIRS * j + h) * P // 2) / (2.0 * math.pi)
+                nc.vector.tensor_scalar_mul(
+                    out=turns[:, h, j : j + 1],
+                    in0=turned[:, 1, 0:1],
+                    scalar1=first if j == 1 else -first,
+                )
 
         table = const.tile([P, PAIRS, 2, 2, SEQ], F32)
 
@@ -160,8 +157,13 @@ def tile_ropemultiheadattention_pa_t_kernel(
             for stage_no in range(3):
                 table_stage(span, h, stage_no, kept)
 
-        mx_ps = pools.enter_context(tc.psum_pool(name="mx_ps", bufs=2))
-        turn_ps = pools.enter_context(tc.psum_pool(name="turn_ps", bufs=3))
+        build_tables(0, 0)
+
+        bias_rows_f32 = const.tile([P, P], F32)
+        nc.vector.tensor_copy(out=bias_rows_f32[:], in_=bias_rows[:])
+        nc.tensor.transpose(turned[:, 0, :], bias_rows_f32[:], ident[:])
+        bias = const.tile([P, 2 * TILES], F32)
+        nc.vector.tensor_copy(out=bias[:], in_=turned[:, 0, 0 : 2 * TILES])
 
         def quantise_x(x_rows):
             grouped = x_mx.tile([P, 4 * TOKENS], BF16, align_bytes=64)
@@ -206,7 +208,7 @@ def tile_ropemultiheadattention_pa_t_kernel(
         def shared_products(banks, span, proj, h):
             cols = slice(span * TOKENS, (span + 1) * TOKENS)
             products = rotated.tile([P, 2, 2, TOKENS], F32)
-            t = tiles * proj + h
+            t = TILES * proj + h
             lower_sb = lifted.tile([P, TOKENS], F32)
             nc.scalar.activation(
                 out=lower_sb[:], in_=banks[0][:], func=ACT.Identity, bias=bias[:, t : t + 1], scale=1.0
@@ -227,7 +229,7 @@ def tile_ropemultiheadattention_pa_t_kernel(
             else:
                 sources = (1,)
             for source in sources:
-                t = tiles * proj + PAIRS * source + h
+                t = TILES * proj + PAIRS * source + h
                 nc.vector.scalar_tensor_tensor(
                     out=products[:, source, :, :],
                     in0=banks[source][:].unsqueeze(1).to_broadcast([P, 2, TOKENS]),
@@ -306,13 +308,14 @@ def tile_ropemultiheadattention_pa_t_kernel(
                 if h == 0:
                     stages[proj] = staging.tile([P, BLOCKS, FEAT], F32, name="stage")
                 turn_back(products_of[i], h, stages[proj], is_summed(i))
-                if h == PAIRS - 1:
+                if h % 2 == 1:
                     rows = outs[proj][batch, span * TOKENS : (span + 1) * TOKENS, :]
-                    nc.sync.dma_start(out=rows.rearrange("(n p) i -> p n i", p=P), in_=stages[proj][:])
+                    rows = rows.rearrange("(n p) i -> p n i", p=P)
+                    for j in range(2):
+                        new = slice((PAIRS * j + h - 1) * P, (PAIRS * j + h + 1) * P)
+                        nc.sync.dma_start(out=rows[:, :, new], in_=stages[proj][:, :, new])
 
-        loaded[1] = load_x(1)
         x_of[0] = quantise_x(loaded[0])
-        build_tables(0, 0)
         front(0)
         build_tables(0, 1)
         for m in range(len(steps) // JOINED):
@@ -327,10 +330,10 @@ def tile_ropemultiheadattention_pa_t_kernel(
                     turn_x(loaded[g + 1], halves[0], place)
                 if place == BLOCKS // 2:
                     x_of[g + 1] = quantise(halves[0])
+            if m + 1 < len(steps) // JOINED:
+                front(m + 1)
             if m + 2 < PAIRS:
                 build_tables(0, m + 2)
             if per_group <= m < per_group + 3 * PAIRS:
                 table_stage(1, (m - per_group) // 3, (m - per_group) % 3, later)
-            if m + 1 < len(steps) // JOINED:
-                front(m + 1)
             back(m)

@@ -44,8 +44,7 @@ def tile_ropemultiheadattention_pa_t_kernel(
         lifted = pools.enter_context(tc.tile_pool(name="lifted", bufs=2))
         staging = pools.enter_context(tc.tile_pool(name="staging", bufs=4))
         keep_ps = pools.enter_context(tc.psum_pool(name="keep_ps", bufs=1))
-        mx_ps = pools.enter_context(tc.psum_pool(name="mx_ps", bufs=2))
-        turn_ps = pools.enter_context(tc.psum_pool(name="turn_ps", bufs=3))
+        turn_ps = pools.enter_context(tc.psum_pool(name="turn_ps", bufs=7))
 
         groups = [(batch, span) for span in range(SPANS) for batch in range(BATCH)]
 
@@ -92,13 +91,9 @@ def tile_ropemultiheadattention_pa_t_kernel(
         nc.tensor.transpose(turned[:, 1, :], ratio_row[:], ident[:])
 
         position = const.tile([P, SEQ], F32)
-        nc.vector.memset(position[:, 0:1], 0.0)
-        width = 1
-        while width < SEQ:
-            nc.vector.tensor_scalar_add(
-                out=position[:, width : 2 * width], in0=position[:, 0:width], scalar1=float(width)
-            )
-            width *= 2
+        nc.gpsimd.iota(
+            position[:], pattern=[[1, SEQ]], base=0, channel_multiplier=0, allow_small_or_imprecise_dtypes=True
+        )
 
         quarter = const.tile([P, 1], F32)
         nc.vector.memset(quarter[:], 0.25)
@@ -188,10 +183,10 @@ def tile_ropemultiheadattention_pa_t_kernel(
             nc.vector.quantize_mx(out=codes[:].bitcast(FP8X4), scales=scales[:], in_=grouped[:])
             return codes, scales
 
-        def project(x_group, proj, h):
+        def project(x_group, proj, h, lifted_soon):
             codes, scales = x_group
-            lower = mx_ps.tile([P, TOKENS], F32)
-            upper = mx_ps.tile([P, TOKENS], F32)
+            lower = turn_ps.tile([P, TOKENS], F32, name="bank", tag="bank")
+            upper = turn_ps.tile([P, TOKENS], F32, name="bank", tag="bank")
             for j, bank in enumerate((lower, upper)):
                 t = PAIRS * j + h
                 nc.tensor.matmul_mx(
@@ -249,7 +244,7 @@ def tile_ropemultiheadattention_pa_t_kernel(
             )
 
         def turn_back(products, h, stage, summed):
-            for j in range(2):
+            for j in (1, 0) if summed else (0, 1):
                 sums = turn_ps.tile([P, BLOCKS, P], F32, name="bank", tag="bank")
                 terms = 1 if (summed and j < SUMMED) else 2
                 for n in range(BLOCKS):
@@ -288,7 +283,7 @@ def tile_ropemultiheadattention_pa_t_kernel(
             members = range(JOINED * m, JOINED * (m + 1))
             for i in members:
                 g, proj, h = steps[i]
-                banks_of[i] = project(x_of[g], proj, h)
+                banks_of[i] = project(x_of[g], proj, h, is_shared(i))
             for i in members:
                 g, proj, h = steps[i]
                 products_of[i] = None

import math
from contextlib import ExitStack

import concourse.mybir as mybir
from concourse.masks import make_identity

F32 = mybir.dt.float32
BF16 = mybir.dt.bfloat16
I32 = mybir.dt.int32
U32 = mybir.dt.uint32
U8 = mybir.dt.uint8
FP8X4 = mybir.dt.float8_e4m3fn_x4
FP4X4 = mybir.dt.float4_e2m1fn_x4
ALU = mybir.AluOpType
ACT = mybir.ActivationFunctionType

P = 128
BATCH, SEQ, DIM, FEAT = 4, 1024, 512, 1024
ROPE_BASE = 10000.0
TOKENS = 512
BLOCKS = TOKENS // P
SPANS = SEQ // TOKENS
TILES = FEAT // P
PAIRS = TILES // 2
WORDS = DIM // 2
SUMMED = 1
JOINED = 2

FLOPS = 2 * BATCH * SEQ * DIM * 2 * FEAT


def tile_ropemultiheadattention_pa_t_kernel(
    tc, x, Wq_words, Wq_scales, bq, Wk_words, Wk_scales, bk, out_0, out_1
):
    nc = tc.nc
    outs = (out_0, out_1)

    with ExitStack() as pools:
        const = pools.enter_context(tc.tile_pool(name="const", bufs=1))
        angle = pools.enter_context(tc.tile_pool(name="angle", bufs=2))
        x_in = pools.enter_context(tc.tile_pool(name="x_in", bufs=3))
        x_mx = pools.enter_context(tc.tile_pool(name="x_mx", bufs=2))
        rotated = pools.enter_context(tc.tile_pool(name="rotated", bufs=4))
        lifted = pools.enter_context(tc.tile_pool(name="lifted", bufs=2))
        staging = pools.enter_context(tc.tile_pool(name="staging", bufs=4))
        keep_ps = pools.enter_context(tc.psum_pool(name="keep_ps", bufs=1))
        turn_ps = pools.enter_context(tc.psum_pool(name="turn_ps", bufs=7))

        groups = [(batch, span) for span in range(SPANS) for batch in range(BATCH)]

        def load_x(g):
            batch, span = groups[g]
            rows = x[batch, span * TOKENS : (span + 1) * TOKENS, :]
            x_rows = x_in.tile([P, BLOCKS, DIM], BF16)
            nc.sync.dma_start(out=x_rows[:], in_=rows.rearrange("(n p) k -> p n k", p=P))
            return x_rows

        loaded = {0: load_x(0)}
        bias_rows = const.tile([P, P], BF16)
        nc.vector.memset(bias_rows[:], 0.0)
        nc.sync.dma_start(out=bias_rows[0:TILES, :], in_=bq.rearrange("(t p) -> t p", p=P))
        nc.sync.dma_start(out=bias_rows[TILES : 2 * TILES, :], in_=bk.rearrange("(t p) -> t p", p=P))
        w_words = const.tile([P, 2, 2 * FEAT], U8, align_bytes=64)
        w_scales = const.tile([P, 2, FEAT], U8, align_bytes=64)
        nc.vector.memset(w_scales[:].bitcast(I32), 0)
        for proj, (words, scales) in enumerate(((Wq_words, Wq_scales), (Wk_words, Wk_scales))):
            nc.sync.dma_start(out=w_words[:, proj, :].bitcast(I32), in_=words[0].bitcast(I32))
            for quad in range(4):
                nc.sync.dma_start(
                    out=w_scales[32 * quad : 32 * quad + 4, proj, :].bitcast(I32),
                    in_=scales[0, 4 * quad : 4 * quad + 4, :].bitcast(I32),
                )
        loaded[1] = load_x(1)

        ident = const.tile([P, P], F32)
        make_identity(nc, ident[:])

        ratio = ROPE_BASE ** (-2.0 / FEAT)
        ratio_row = const.tile([P, P], F32)
        nc.vector.memset(ratio_row[:, 0:2], 1.0)
        width = 2
        while width < P:
            nc.vector.tensor_scalar_mul(
                out=ratio_row[:, width : 2 * width],
                in0=ratio_row[:, 0:width],
                scalar1=ratio ** (width // 2),
            )
            width *= 2

        turned = keep_ps.tile([P, 2, P], F32)
        nc.tensor.transpose(turned[:, 1, :], ratio_row[:], ident[:])

        position = const.tile([P, SEQ], F32)
        nc.gpsimd.iota(
            position[:], pattern=[[1, SEQ]], base=0, channel_multiplier=0, allow_small_or_imprecise_dtypes=True
        )

        quarter = const.tile([P, 1], F32)
        nc.vector.memset(quarter[:], 0.25)
        quarter_turn = const.tile([P, 1], F32)
        nc.vector.tensor_scalar_mul(out=quarter_turn[:], in0=quarter[:], scalar1=2.0 * math.pi)

        turns = const.tile([P, PAIRS, 2], F32)
        for h in range(PAIRS):
            for j in range(2):
                first = ratio ** ((PAIRS * j + h) * P // 2) / (2.0 * math.pi)
                nc.vector.tensor_scalar_mul(
                    out=turns[:, h, j : j + 1],
                    in0=turned[:, 1, 0:1],
                    scalar1=first if j == 1 else -first,
                )

        table = const.tile([P, PAIRS, 2, 2, SEQ], F32)

        def table_stage(span, h, stage_no, kept):
            cols = slice(span * TOKENS, (span + 1) * TOKENS)
            if stage_no == 0:
                whole = angle.tile([P, 2, TOKENS], I32)
                part = angle.tile([P, 2, TOKENS], F32)
                for j in range(2):
                    nc.vector.tensor_scalar_mul(
                        out=whole[:, j, :], in0=position[:, cols], scalar1=turns[:, h, j : j + 1]
                    )
                    nc.vector.scalar_tensor_tensor(
                        out=part[:, j, :],
                        in0=position[:, cols],
                        scalar=turns[:, h, j : j + 1],
                        in1=whole[:, j, :],
                        op0=ALU.mult,
                        op1=ALU.subtract,
                    )
                for j in range(2):
                    nc.scalar.activation(
                        out=table[:, h, 1 - j, j, cols], in_=part[:, j, :], func=ACT.Sin, scale=2.0 * math.pi
                    )
                kept[0] = part
            if stage_no == 1:
                size = angle.tile([P, 2, TOKENS], F32)
                nc.scalar.activation(out=size[:], in_=kept[0][:], func=ACT.Abs)
                kept[1] = size
            if stage_no == 2:
                nc.scalar.activation(
                    out=table[:, h].rearrange("p a b s -> p (a b) s")[:, 0:4:3, cols],
                    in_=kept[1][:],
                    func=ACT.Sin,
                    scale=-2.0 * math.pi,
                    bias=quarter_turn[:, 0:1],
                )

        def build_tables(span, h):
            kept = {}
            for stage_no in range(3):
                table_stage(span, h, stage_no, kept)

        build_tables(0, 0)

        bias_rows_f32 = const.tile([P, P], F32)
        nc.vector.tensor_copy(out=bias_rows_f32[:], in_=bias_rows[:])
        nc.tensor.transpose(turned[:, 0, :], bias_rows_f32[:], ident[:])
        bias = const.tile([P, 2 * TILES], F32)
        nc.vector.tensor_copy(out=bias[:], in_=turned[:, 0, 0 : 2 * TILES])

        def quantise_x(x_rows):
            grouped = x_mx.tile([P, 4 * TOKENS], BF16, align_bytes=64)
            for c in range(BLOCKS // 2):
                turn_x(x_rows, grouped, c)
            return quantise(grouped)

        def turn_x(x_rows, grouped, c):
            grouped_words = grouped[:].bitcast(F32).rearrange(
                "p (c n m u) -> p c n m u", c=BLOCKS // 2, n=2, u=2
            )
            planes = turn_ps.tile([P, 2, 2, P], F32, name="bank", tag="bank")
            for n in range(2):
                words = x_rows[:, 2 * c + n, :].bitcast(F32)
                for u in range(2):
                    nc.tensor.transpose(planes[:, n, u, :], words[:, u:WORDS:2], ident[:])
            nc.scalar.copy(out=grouped_words[:, c], in_=planes[:].rearrange("p n u m -> p n m u"))

        def quantise(grouped):
            codes = x_mx.tile([P, TOKENS], U32, align_bytes=64)
            scales = x_mx.tile([P, TOKENS], U8, align_bytes=64)
            nc.vector.quantize_mx(out=codes[:].bitcast(FP8X4), scales=scales[:], in_=grouped[:])
            return codes, scales

        def project(x_group, proj, h, lifted_soon):
            codes, scales = x_group
            lower = turn_ps.tile([P, TOKENS], F32, name="bank", tag="bank")
            upper = turn_ps.tile([P, TOKENS], F32, name="bank", tag="bank")
            for j, bank in enumerate((lower, upper)):
                t = PAIRS * j + h
                nc.tensor.matmul_mx(
                    out=bank[:],
                    lhsT=w_words[:, proj, 2 * P * t : 2 * P * (t + 1)].bitcast(FP4X4),
                    lhsT_scale=w_scales[:, proj, P * t : P * (t + 1)],
                    rhs=codes[:].bitcast(FP8X4),
                    rhs_scale=scales[:],
                    start=True,
                    stop=True,
                )
            return lower, upper

        def shared_products(banks, span, proj, h):
            cols = slice(span * TOKENS, (span + 1) * TOKENS)
            products = rotated.tile([P, 2, 2, TOKENS], F32)
            t = TILES * proj + h
            lower_sb = lifted.tile([P, TOKENS], F32)
            nc.scalar.activation(
                out=lower_sb[:], in_=banks[0][:], func=ACT.Identity, bias=bias[:, t : t + 1], scale=1.0
            )
            nc.gpsimd.tensor_tensor(
                out=products[:, 0, :, :],
                in0=lower_sb[:].unsqueeze(1).to_broadcast([P, 2, TOKENS]),
                in1=table[:, h, 0, :, cols],
                op=ALU.mult,
            )
            return products

        def vector_products(banks, span, proj, h, products):
            cols = slice(span * TOKENS, (span + 1) * TOKENS)
            sources = (0, 1)
            if products is None:
                products = rotated.tile([P, 2, 2, TOKENS], F32)
            else:
                sources = (1,)
            for source in sources:
                t = TILES * proj + PAIRS * source + h
                nc.vector.scalar_tensor_tensor(
                    out=products[:, source, :, :],
                    in0=banks[source][:].unsqueeze(1).to_broadcast([P, 2, TOKENS]),
                    scalar=turned[:, 0, t : t + 1],
                    in1=table[:, h, source, :, cols],
                    op0=ALU.add,
                    op1=ALU.mult,
                )
            return products

        def add_halves(products):
            nc.gpsimd.tensor_tensor(
                out=products[:, 0, 0:SUMMED, :],
                in0=products[:, 0, 0:SUMMED, :],
                in1=products[:, 1, 0:SUMMED, :],
                op=ALU.add,
            )

        def turn_back(products, h, stage, summed):
            for j in (1, 0) if summed else (0, 1):
                sums = turn_ps.tile([P, BLOCKS, P], F32, name="bank", tag="bank")
                terms = 1 if (summed and j < SUMMED) else 2
                for n in range(BLOCKS):
                    for source in range(terms):
                        nc.tensor.matmul(
                            out=sums[:, n, :],
                            lhsT=products[:, source, j, n * P : (n + 1) * P],
                            rhs=ident[:],
                            is_transpose=True,
                            start=(source == 0),
                            stop=(source == terms - 1),
                        )
                t = PAIRS * j + h
                nc.scalar.copy(out=stage[:, :, t * P : (t + 1) * P], in_=sums[:])

        steps = [(0, proj, h) for h in range(PAIRS) for proj in range(2)]
        steps.extend(
            (g, proj, h) for g in range(1, len(groups)) for proj in range(2) for h in range(PAIRS)
        )
        per_group = 2 * PAIRS // JOINED

        def is_shared(i):
            return i % 2 == 0

        def is_summed(i):
            return i % 2 == 1

        x_of = {}
        banks_of = {}
        products_of = {}
        stages = {}
        halves = {}
        later = {}

        def front(m):
            members = range(JOINED * m, JOINED * (m + 1))
            for i in members:
                g, proj, h = steps[i]
                banks_of[i] = project(x_of[g], proj, h, is_shared(i))
            for i in members:
                g, proj, h = steps[i]
                products_of[i] = None
                if is_shared(i):
                    products_of[i] = shared_products(banks_of[i], groups[g][1], proj, h)
            for i in members:
                g, proj, h = steps[i]
                products_of[i] = vector_products(banks_of[i], groups[g][1], proj, h, products_of[i])
            for i in members:
                if is_summed(i):
                    add_halves(products_of[i])

        def back(m):
            for i in range(JOINED * m, JOINED * (m + 1)):
                g, proj, h = steps[i]
                batch, span = groups[g]
                if h == 0:
                    stages[proj] = staging.tile([P, BLOCKS, FEAT], F32, name="stage")
                turn_back(products_of[i], h, stages[proj], is_summed(i))
                if h % 2 == 1:
                    rows = outs[proj][batch, span * TOKENS : (span + 1) * TOKENS, :]
                    rows = rows.rearrange("(n p) i -> p n i", p=P)
                    for j in range(2):
                        new = slice((PAIRS * j + h - 1) * P, (PAIRS * j + h + 1) * P)
                        nc.sync.dma_start(out=rows[:, :, new], in_=stages[proj][:, :, new])

        x_of[0] = quantise_x(loaded[0])
        front(0)
        build_tables(0, 1)
        for m in range(len(steps) // JOINED):
            g = steps[JOINED * m][0]
            place = m % per_group
            if place == 0 and g + 2 < len(groups):
                loaded[g + 2] = load_x(g + 2)
            if g + 1 < len(groups):
                if place == 0:
                    halves[0] = x_mx.tile([P, 4 * TOKENS], BF16, align_bytes=64, name="grouped")
                if place < BLOCKS // 2:
                    turn_x(loaded[g + 1], halves[0], place)
                if place == BLOCKS // 2:
                    x_of[g + 1] = quantise(halves[0])
            if m + 1 < len(steps) // JOINED:
                front(m + 1)
            if m + 2 < PAIRS:
                build_tables(0, m + 2)
            if per_group <= m < per_group + 3 * PAIRS:
                table_stage(1, (m - per_group) // 3, (m - per_group) % 3, later)
            back(m)
